import numpy as np
import ml_dtypes


def mxq(x, axis, fmt="e4m3"):
    dtype, down = {"e4m3": (ml_dtypes.float8_e4m3fn, 7), "e5m2": (ml_dtypes.float8_e5m2, 14)}[fmt]
    v = np.moveaxis(np.asarray(x, np.float32).astype(ml_dtypes.bfloat16).astype(np.float64), axis, -1)
    blocks = v.reshape(v.shape[:-1] + (-1, 32))
    amax = np.abs(blocks).max(-1, keepdims=True)
    byte = np.maximum(np.where(amax > 0, np.frexp(amax)[1] - 1 + 127, 0) - down, 1)
    scale = np.exp2(byte - 127.0)
    codes = (blocks / scale).astype(np.float32).astype(dtype).astype(np.float64)
    return np.moveaxis((codes * scale).reshape(v.shape), -1, axis)


WIDE = False


def mx_kscale(k):
    if not WIDE:
        return np.ones(k)
    levels = np.array([10, -10, 5, -5, 0])
    if k % 512:
        return np.exp2(np.random.permutation(np.resize(levels, k // 32))).repeat(32)
    a = np.empty((k // 512, 16))
    for p in range(k // 512):
        a[p, :8] = np.random.permutation(np.resize(levels, 8))
        for g in range(8):
            far = levels[np.abs(levels - a[p, g]) >= 10]
            a[p, g + 8] = far[np.random.randint(len(far))]
    return np.exp2(a.ravel()).repeat(32)


BF16 = ml_dtypes.bfloat16


def bf(x):
    return np.asarray(x, np.float32).astype(BF16)


def f64(x):
    return np.asarray(x).astype(np.float64)


NB, D1, KB, P, Q, LB, S = 4, 256, 8, 512, 512, 8, 512
D2 = KB * P
R = KB * Q // LB
DO = S * LB


def _blockdiag_butterfly_multiply(x, w1, w2):
    B, n = x.shape
    k, q, p = w1.shape
    l, s, r = w2.shape
    x_r = x.reshape(B, k, p).transpose(1, 0, 2)
    out1 = mxq(x_r, 2, "e4m3") @ mxq(w1, 2, "e4m3").transpose(0, 2, 1)
    out1 = out1.transpose(1, 0, 2).reshape(B, r, l).transpose(2, 0, 1)
    out2 = mxq(out1, 2, "e4m3") @ mxq(w2, 2, "e4m3").transpose(0, 2, 1)
    return out2.transpose(1, 2, 0).reshape(B, s * l)


def setup_inputs():
    s = mx_kscale(P)
    t = mx_kscale(R)
    tf = np.repeat(t, LB).reshape(KB, Q)
    return {"x": bf(np.random.standard_normal((NB, D1, D2)) * np.tile(s, KB)),
            "factorL": bf(np.random.standard_normal((KB, Q, P)) / np.sqrt(P) / s * tf[:, :, None]),
            "factorR": bf(np.random.standard_normal((LB, S, R)) / np.sqrt(R) / t),
            "bias": bf(np.random.standard_normal(DO) * 0.5)}


def reference(x, factorL, factorR, bias):
    b, d1, d2 = x.shape
    out = _blockdiag_butterfly_multiply(f64(x).reshape(-1, d2), f64(factorL), f64(factorR))
    out = out.reshape(b, d1, -1)
    return out + f64(bias)

@@ -1,0 +1,264 @@
+from contextlib import ExitStack
+
+import concourse.mybir as mybir
+from concourse.masks import make_identity
+
+F32 = mybir.dt.float32
+BF16 = mybir.dt.bfloat16
+U32 = mybir.dt.uint32
+U8 = mybir.dt.uint8
+FP8X4 = mybir.dt.float8_e4m3fn_x4
+ADD = mybir.AluOpType.add
+
+H_BANK = F32
+
+P = 128
+NBT = 8
+NK = 8
+NL = 8
+FLOPS = 2 * 2 * 1024 * 4096 * 512
+LEAD = 2
+
+
+def tile_butterflyblocksparselinear_kernel(tc, x, factorL, factorR, bias, out):
+    nc = tc.nc
+    xf = x.flatten_outer_dims()
+    of = out.flatten_outer_dims()
+    fl_rows = factorL.rearrange("k q p -> (k q) p").rearrange("(t r l) p -> t r l p", r=P, l=8)
+    fr_rows = factorR.rearrange("l s r -> (l s) r").rearrange("(c g s) r -> c s g r", g=8, s=P)
+
+    with ExitStack() as ctx:
+        const = ctx.enter_context(tc.tile_pool(name="const", bufs=1))
+        wraw_pool = ctx.enter_context(tc.tile_pool(name="wraw", bufs=4))
+        wg_pool = ctx.enter_context(tc.tile_pool(name="wg", bufs=2))
+        xraw_pool = ctx.enter_context(tc.tile_pool(name="xraw", bufs=4))
+        two = ctx.enter_context(tc.tile_pool(name="two", bufs=2))
+        three = ctx.enter_context(tc.tile_pool(name="three", bufs=3))
+        o_pool = ctx.enter_context(tc.tile_pool(name="o", bufs=4))
+        psum = ctx.enter_context(tc.psum_pool(name="psum", bufs=8))
+        ctx.enter_context(tc.manual_schedule())
+
+        act = nc.scalar.copy
+        dve = nc.vector.tensor_copy
+
+        warm_in = const.tile([P, 1], F32, name="warm_in", tag="warm_in")
+        warm_out = const.tile([P, 1], F32, name="warm_out", tag="warm_out")
+        nc.vector.memset(warm_in[:], 0.0)
+        nc.scalar.copy(out=warm_out[:], in_=warm_in[:])
+        ident = const.tile([P, P], F32, name="ident", tag="ident")
+        make_identity(nc, ident[:])
+        perm = const.tile([P, P], F32, name="perm", tag="perm")
+        for k2 in range(2):
+            nc.vector.tensor_copy(
+                out=perm[:, 64 * k2 : 64 * k2 + 64].rearrange("p (u c e) -> p u c e", u=2, e=2),
+                in_=ident[:, 64 * k2 : 64 * k2 + 64].rearrange("p (c u e) -> p u c e", u=2, e=2),
+            )
+        bias_bc = const.tile([P, 512, 8], BF16, name="bias_bc", tag="bias_bc")
+        fl_q = const.tile([P, NK, 512], U32, name="fl_q", tag="fl_q", align_bytes=64)
+        fl_s = const.tile([P, NK, 512], U8, name="fl_s", tag="fl_s", align_bytes=64)
+        fr_q = const.tile([P, NL, 512], U32, name="fr_q", tag="fr_q", align_bytes=64)
+        fr_s = const.tile([P, NL, 512], U8, name="fr_s", tag="fr_s", align_bytes=64)
+
+        x_raw = {}
+        x_g = {}
+        x_q = {}
+        x_s = {}
+        w_raw = {}
+        g_nat = {}
+        g_g = {}
+        g_q = {}
+        g_s = {}
+        o_sb = {}
+
+        def load_x(n, pieces):
+            x_raw[n] = xraw_pool.tile([P, 4096], BF16, name="x_raw%d" % n, tag="x_raw")
+            w = 4096 // pieces
+            for c in range(pieces):
+                nc.sync.dma_start(
+                    out=x_raw[n][:, c * w : (c + 1) * w],
+                    in_=xf[P * n : P * (n + 1), c * w : (c + 1) * w],
+                )
+
+        def load_w(key, rows):
+            w_raw[key] = wraw_pool.tile([P, 8, 512], BF16, name="w_raw_%s" % key, tag="w_raw")
+            nc.sync.dma_start(out=w_raw[key][:], in_=rows)
+
+        def quantize(src, codes, scales):
+            nc.vector.quantize_mx(out=codes.bitcast(FP8X4), scales=scales, in_=src)
+
+        def prep_fl(rt):
+            words = w_raw["fl%d" % rt][:].bitcast(F32)
+            grouped = wg_pool.tile([P, 2, 8, 64, 4], BF16, name="fl_g%d" % rt, tag="w_g", align_bytes=64)
+            gw = grouped[:].bitcast(F32)
+            for ll in range(4):
+                tp = psum.tile([P, 4, P], F32, name="tp_fl%d_%d" % (rt, ll), tag="ps")
+                for l2 in range(2):
+                    for u in range(2):
+                        nc.tensor.transpose(tp[:, 2 * l2 + u, :], words[:, 2 * ll + l2, u:256:2], perm[:])
+                act(
+                    out=gw[:, :, 2 * ll : 2 * ll + 2, :, :],
+                    in_=tp[:].rearrange("p (l u) (k n) -> p k l n u", u=2, k=2),
+                )
+            return grouped
+
+        def quant_fl(rt, grouped):
+            for k2 in range(2):
+                quantize(
+                    grouped[:, k2].rearrange("p l n t -> p (l n t)"),
+                    fl_q[:, 2 * rt + k2, :],
+                    fl_s[:, 2 * rt + k2, :],
+                )
+
+        def prep_fr(c):
+            words = w_raw["fr%d" % c][:].bitcast(F32)
+            grouped = wg_pool.tile([P, 2, 512, 4], BF16, name="fr_g%d" % c, tag="w_g", align_bytes=64)
+            gw = grouped[:].bitcast(F32)
+            for l2 in range(2):
+                for ah in range(2):
+                    tp = psum.tile([P, 4, P], F32, name="tp_fr%d_%d_%d" % (c, l2, ah), tag="ps")
+                    for a2 in range(2):
+                        for u in range(2):
+                            nc.tensor.transpose(
+                                tp[:, 2 * a2 + u, :], words[:, 4 * l2 + 2 * ah + a2, u:256:2], ident[:]
+                            )
+                    act(
+                        out=gw[:, l2, 256 * ah : 256 * ah + 256, :].rearrange("p (a s) u -> p a s u", a=2),
+                        in_=tp[:].rearrange("p (a u) s -> p a s u", u=2),
+                    )
+            return grouped
+
+        def quant_fr(c, grouped):
+            for l2 in range(2):
+                quantize(
+                    grouped[:, l2].rearrange("p s t -> p (s t)"),
+                    fr_q[:, 2 * c + l2, :],
+                    fr_s[:, 2 * c + l2, :],
+                )
+
+        def turn_x(n, engines):
+            words = x_raw[n][:].bitcast(F32)
+            x_g[n] = two.tile([P, NK, P, 4], BF16, name="x_g%d" % n, tag="x_g", align_bytes=64)
+            x_q[n] = three.tile([P, NK * P], U32, name="x_q%d" % n, tag="x_q", align_bytes=64)
+            x_s[n] = three.tile([P, NK * P], U8, name="x_s%d" % n, tag="x_s", align_bytes=64)
+            gw = x_g[n][:].bitcast(F32)
+            for kk in range(4):
+                tp = psum.tile([P, 4, P], F32, name="tp_x%d_%d" % (n, kk), tag="ps")
+                for k2 in range(2):
+                    for u in range(2):
+                        k = 2 * kk + k2
+                        nc.tensor.transpose(tp[:, 2 * k2 + u, :], words[:, 256 * k + u : 256 * (k + 1) : 2], ident[:])
+                engines[kk](
+                    out=gw[:, 2 * kk : 2 * kk + 2, :, :],
+                    in_=tp[:].rearrange("p (k u) b -> p k b u", u=2),
+                )
+
+        def quant_x(n):
+            quantize(x_g[n][:].rearrange("p k b t -> p (k b t)"), x_q[n][:], x_s[n][:])
+
+        def stage1(n, k, eng):
+            if k == 0:
+                g_nat[n] = two.tile([P, 16, NK, 32], BF16, name="g_nat%d" % n, tag="g_nat")
+            h_ps = psum.tile([P, 512], H_BANK, name="h_ps%d_%d" % (n, k), tag="ps")
+            nc.tensor.matmul_mx(
+                out=h_ps[:],
+                lhsT=x_q[n][:, P * k : P * (k + 1)].bitcast(FP8X4),
+                lhsT_scale=x_s[n][:, P * k : P * (k + 1)],
+                rhs=fl_q[:, k, :].bitcast(FP8X4),
+                rhs_scale=fl_s[:, k, :],
+                start=True,
+                stop=True,
+            )
+            eng(out=g_nat[n][:, :, k, :], in_=h_ps[:].rearrange("p (a c) -> p a c", c=32))
+
+        def turn_h(n):
+            words = g_nat[n][:].rearrange("p a k c -> p (a k c)").bitcast(F32)
+            g_g[n] = two.tile([P, NL, P, 4], BF16, name="g_g%d" % n, tag="g_g", align_bytes=64)
+            g_q[n] = two.tile([P, NL * P], U32, name="g_q%d" % n, tag="g_q", align_bytes=64)
+            g_s[n] = two.tile([P, NL * P], U8, name="g_s%d" % n, tag="g_s", align_bytes=64)
+            gw = g_g[n][:].bitcast(F32)
+            for ll in range(4):
+                tp = psum.tile([P, 4, P], F32, name="tp_h%d_%d" % (n, ll), tag="ps")
+                for s in range(4):
+                    nc.tensor.transpose(tp[:, s, :], words[:, P * (4 * ll + s) : P * (4 * ll + s + 1)], ident[:])
+                act(
+                    out=gw[:, 2 * ll : 2 * ll + 2, :, :],
+                    in_=tp[:].rearrange("p (l u) b -> p l b u", u=2),
+                )
+                if ll % 2 == 1:
+                    h = ll // 2
+                    quantize(
+                        g_g[n][:, 4 * h : 4 * h + 4, :, :].rearrange("p l b t -> p (l b t)"),
+                        g_q[n][:, 512 * h : 512 * h + 512],
+                        g_s[n][:, 512 * h : 512 * h + 512],
+                    )
+
+        def stage2(n, j):
+            a = j // 2
+            lh = j % 2
+            if lh == 0:
+                o_sb[n] = o_pool.tile([P, P, 8], F32, name="o_sb%d_%d" % (n, a), tag="o_sb")
+            y_ps = psum.tile([P, 4, P], F32, name="y_ps%d_%d" % (n, j), tag="ps")
+            for l4 in range(4):
+                l = 4 * lh + l4
+                nc.tensor.matmul_mx(
+                    out=y_ps[:, l4, :],
+                    lhsT=g_q[n][:, P * l : P * (l + 1)].bitcast(FP8X4),
+                    lhsT_scale=g_s[n][:, P * l : P * (l + 1)],
+                    rhs=fr_q[:, l, P * a : P * (a + 1)].bitcast(FP8X4),
+                    rhs_scale=fr_s[:, l, P * a : P * (a + 1)],
+                    start=True,
+                    stop=True,
+                )
+            nc.vector.tensor_tensor(
+                out=o_sb[n][:, :, 4 * lh : 4 * lh + 4],
+                in0=y_ps[:].rearrange("p l s -> p s l"),
+                in1=bias_bc[:, P * a : P * (a + 1), 4 * lh : 4 * lh + 4],
+                op=ADD,
+            )
+            if lh == 1:
+                nc.sync.dma_start(
+                    out=of[P * n : P * (n + 1), 1024 * a : 1024 * (a + 1)],
+                    in_=o_sb[n][:].rearrange("p s l -> p (s l)"),
+                )
+
+        load_x(0, 2)
+        for rt in range(4):
+            load_w("fl%d" % rt, fl_rows[rt])
+        load_x(1, 1)
+
+        turn_x(0, [act, dve, act, dve])
+        quant_x(0)
+        for rt in range(4):
+            grouped = prep_fl(rt)
+            load_w("fr%d" % rt, fr_rows[rt])
+            quant_fl(rt, grouped)
+        load_x(2, 1)
+        nc.sync.dma_start(out=bias_bc[:].rearrange("p s l -> p (s l)"), in_=bias.partition_broadcast(P))
+        load_x(3, 1)
+        turn_x(1, [act, dve, act, dve])
+        quant_x(1)
+        load_x(4, 1)
+        load_x(5, 1)
+        for k in range(4):
+            stage1(0, k, act if k % 2 == 0 else dve)
+        grouped = prep_fr(0)
+        quant_fr(0, grouped)
+        for k in range(4, 8):
+            stage1(0, k, act if k % 2 == 0 else dve)
+        for c in range(1, 4):
+            grouped = prep_fr(c)
+            quant_fr(c, grouped)
+
+        for i in range(NBT):
+            turn_h(i)
+            if i + 2 < NBT:
+                turn_x(i + 2, [act, dve, act, dve])
+                if i + 6 < NBT:
+                    load_x(i + 6, 1)
+            for j in range(8 + LEAD):
+                if j < 8 and i + 1 < NBT:
+                    stage1(i + 1, j, act)
+                if j >= LEAD:
+                    stage2(i, j - LEAD)
+                    if i + 2 < NBT and j - LEAD == 2:
+                        quant_x(i + 2)

@@ -18,6 +18,8 @@ NK = 8
 NL = 8
 FLOPS = 2 * 2 * 1024 * 4096 * 512
 LEAD = 2
+WARM_UP = 6
+KEEP_N = 256
 
 
 def tile_butterflyblocksparselinear_kernel(tc, x, factorL, factorR, bias, out):
@@ -43,6 +45,8 @@ def tile_butterflyblocksparselinear_kernel(tc, x, factorL, factorR, bias, out):
 
         warm_in = const.tile([P, 1], F32, name="warm_in", tag="warm_in")
         warm_out = const.tile([P, 1], F32, name="warm_out", tag="warm_out")
+        zeros = const.tile([P, 512], BF16, name="zeros", tag="zeros")
+        nc.vector.memset(zeros[:], 0.0)
         nc.vector.memset(warm_in[:], 0.0)
         nc.scalar.copy(out=warm_out[:], in_=warm_in[:])
         ident = const.tile([P, P], F32, name="ident", tag="ident")
@@ -70,6 +74,9 @@ def tile_butterflyblocksparselinear_kernel(tc, x, factorL, factorR, bias, out):
         g_s = {}
         o_sb = {}
 
+        def dummy(bank, width):
+            nc.tensor.matmul(out=bank[:, 0:width], lhsT=zeros[:, 0:P], rhs=zeros[:, 0:width], start=True, stop=True)
+
         def load_x(n, pieces):
             x_raw[n] = xraw_pool.tile([P, 4096], BF16, name="x_raw%d" % n, tag="x_raw")
             w = 4096 // pieces
@@ -90,12 +97,14 @@ def tile_butterflyblocksparselinear_kernel(tc, x, factorL, factorR, bias, out):
             words = w_raw["fl%d" % rt][:].bitcast(F32)
             grouped = wg_pool.tile([P, 2, 8, 64, 4], BF16, name="fl_g%d" % rt, tag="w_g", align_bytes=64)
             gw = grouped[:].bitcast(F32)
+            idle = psum.tile([P, 512], F32, name="idle_fl%d" % rt, tag="ps")
             for ll in range(4):
                 tp = psum.tile([P, 4, P], F32, name="tp_fl%d_%d" % (rt, ll), tag="ps")
                 for l2 in range(2):
                     for u in range(2):
                         nc.tensor.transpose(tp[:, 2 * l2 + u, :], words[:, 2 * ll + l2, u:256:2], perm[:])
-                act(
+                dummy(idle, KEEP_N)
+                (dve if ll == 1 else act)(
                     out=gw[:, :, 2 * ll : 2 * ll + 2, :, :],
                     in_=tp[:].rearrange("p (l u) (k n) -> p k l n u", u=2, k=2),
                 )
@@ -121,7 +130,7 @@ def tile_butterflyblocksparselinear_kernel(tc, x, factorL, factorR, bias, out):
                             nc.tensor.transpose(
                                 tp[:, 2 * a2 + u, :], words[:, 4 * l2 + 2 * ah + a2, u:256:2], ident[:]
                             )
-                    act(
+                    (dve if (l2, ah) == (0, 1) else act)(
                         out=gw[:, l2, 256 * ah : 256 * ah + 256, :].rearrange("p (a s) u -> p a s u", a=2),
                         in_=tp[:].rearrange("p (a u) s -> p a s u", u=2),
                     )
@@ -135,18 +144,22 @@ def tile_butterflyblocksparselinear_kernel(tc, x, factorL, factorR, bias, out):
                     fr_s[:, 2 * c + l2, :],
                 )
 
-        def turn_x(n, engines):
+        def turn_x(n, engines, keep):
             words = x_raw[n][:].bitcast(F32)
             x_g[n] = two.tile([P, NK, P, 4], BF16, name="x_g%d" % n, tag="x_g", align_bytes=64)
             x_q[n] = three.tile([P, NK * P], U32, name="x_q%d" % n, tag="x_q", align_bytes=64)
             x_s[n] = three.tile([P, NK * P], U8, name="x_s%d" % n, tag="x_s", align_bytes=64)
             gw = x_g[n][:].bitcast(F32)
+            if keep:
+                idle = psum.tile([P, 512], F32, name="idle_x%d" % n, tag="ps")
             for kk in range(4):
                 tp = psum.tile([P, 4, P], F32, name="tp_x%d_%d" % (n, kk), tag="ps")
                 for k2 in range(2):
                     for u in range(2):
                         k = 2 * kk + k2
                         nc.tensor.transpose(tp[:, 2 * k2 + u, :], words[:, 256 * k + u : 256 * (k + 1) : 2], ident[:])
+                if keep:
+                    dummy(idle, KEEP_N)
                 engines[kk](
                     out=gw[:, 2 * kk : 2 * kk + 2, :, :],
                     in_=tp[:].rearrange("p (k u) b -> p k b u", u=2),
@@ -226,7 +239,10 @@ def tile_butterflyblocksparselinear_kernel(tc, x, factorL, factorR, bias, out):
             load_w("fl%d" % rt, fl_rows[rt])
         load_x(1, 1)
 
-        turn_x(0, [act, dve, act, dve])
+        first = psum.tile([P, 512], F32, name="first", tag="ps")
+        for w in range(WARM_UP):
+            dummy(first, 512)
+        turn_x(0, [act, dve, act, dve], True)
         quant_x(0)
         for rt in range(4):
             grouped = prep_fl(rt)
@@ -235,24 +251,20 @@ def tile_butterflyblocksparselinear_kernel(tc, x, factorL, factorR, bias, out):
         load_x(2, 1)
         nc.sync.dma_start(out=bias_bc[:].rearrange("p s l -> p (s l)"), in_=bias.partition_broadcast(P))
         load_x(3, 1)
-        turn_x(1, [act, dve, act, dve])
+        turn_x(1, [act, dve, act, dve], True)
         quant_x(1)
         load_x(4, 1)
         load_x(5, 1)
-        for k in range(4):
-            stage1(0, k, act if k % 2 == 0 else dve)
-        grouped = prep_fr(0)
-        quant_fr(0, grouped)
-        for k in range(4, 8):
-            stage1(0, k, act if k % 2 == 0 else dve)
-        for c in range(1, 4):
+        for c in range(4):
             grouped = prep_fr(c)
             quant_fr(c, grouped)
+            stage1(0, 2 * c, act)
+            stage1(0, 2 * c + 1, dve)
 
         for i in range(NBT):
             turn_h(i)
             if i + 2 < NBT:
-                turn_x(i + 2, [act, dve, act, dve])
+                turn_x(i + 2, [act, dve, act, dve], False)
                 if i + 6 < NBT:
                     load_x(i + 6, 1)
             for j in range(8 + LEAD):

@@ -18,8 +18,6 @@ NK = 8
 NL = 8
 FLOPS = 2 * 2 * 1024 * 4096 * 512
 LEAD = 2
-WARM_UP = 6
-KEEP_N = 256
 
 
 def tile_butterflyblocksparselinear_kernel(tc, x, factorL, factorR, bias, out):
@@ -45,8 +43,6 @@ def tile_butterflyblocksparselinear_kernel(tc, x, factorL, factorR, bias, out):
 
         warm_in = const.tile([P, 1], F32, name="warm_in", tag="warm_in")
         warm_out = const.tile([P, 1], F32, name="warm_out", tag="warm_out")
-        zeros = const.tile([P, 512], BF16, name="zeros", tag="zeros")
-        nc.vector.memset(zeros[:], 0.0)
         nc.vector.memset(warm_in[:], 0.0)
         nc.scalar.copy(out=warm_out[:], in_=warm_in[:])
         ident = const.tile([P, P], F32, name="ident", tag="ident")
@@ -74,9 +70,6 @@ def tile_butterflyblocksparselinear_kernel(tc, x, factorL, factorR, bias, out):
         g_s = {}
         o_sb = {}
 
-        def dummy(bank, width):
-            nc.tensor.matmul(out=bank[:, 0:width], lhsT=zeros[:, 0:P], rhs=zeros[:, 0:width], start=True, stop=True)
-
         def load_x(n, pieces):
             x_raw[n] = xraw_pool.tile([P, 4096], BF16, name="x_raw%d" % n, tag="x_raw")
             w = 4096 // pieces
@@ -97,14 +90,12 @@ def tile_butterflyblocksparselinear_kernel(tc, x, factorL, factorR, bias, out):
             words = w_raw["fl%d" % rt][:].bitcast(F32)
             grouped = wg_pool.tile([P, 2, 8, 64, 4], BF16, name="fl_g%d" % rt, tag="w_g", align_bytes=64)
             gw = grouped[:].bitcast(F32)
-            idle = psum.tile([P, 512], F32, name="idle_fl%d" % rt, tag="ps")
             for ll in range(4):
                 tp = psum.tile([P, 4, P], F32, name="tp_fl%d_%d" % (rt, ll), tag="ps")
                 for l2 in range(2):
                     for u in range(2):
                         nc.tensor.transpose(tp[:, 2 * l2 + u, :], words[:, 2 * ll + l2, u:256:2], perm[:])
-                dummy(idle, KEEP_N)
-                (dve if ll == 1 else act)(
+                act(
                     out=gw[:, :, 2 * ll : 2 * ll + 2, :, :],
                     in_=tp[:].rearrange("p (l u) (k n) -> p k l n u", u=2, k=2),
                 )
@@ -130,7 +121,7 @@ def tile_butterflyblocksparselinear_kernel(tc, x, factorL, factorR, bias, out):
                             nc.tensor.transpose(
                                 tp[:, 2 * a2 + u, :], words[:, 4 * l2 + 2 * ah + a2, u:256:2], ident[:]
                             )
-                    (dve if (l2, ah) == (0, 1) else act)(
+                    act(
                         out=gw[:, l2, 256 * ah : 256 * ah + 256, :].rearrange("p (a s) u -> p a s u", a=2),
                         in_=tp[:].rearrange("p (a u) s -> p a s u", u=2),
                     )
@@ -144,22 +135,18 @@ def tile_butterflyblocksparselinear_kernel(tc, x, factorL, factorR, bias, out):
                     fr_s[:, 2 * c + l2, :],
                 )
 
-        def turn_x(n, engines, keep):
+        def turn_x(n, engines):
             words = x_raw[n][:].bitcast(F32)
             x_g[n] = two.tile([P, NK, P, 4], BF16, name="x_g%d" % n, tag="x_g", align_bytes=64)
             x_q[n] = three.tile([P, NK * P], U32, name="x_q%d" % n, tag="x_q", align_bytes=64)
             x_s[n] = three.tile([P, NK * P], U8, name="x_s%d" % n, tag="x_s", align_bytes=64)
             gw = x_g[n][:].bitcast(F32)
-            if keep:
-                idle = psum.tile([P, 512], F32, name="idle_x%d" % n, tag="ps")
             for kk in range(4):
                 tp = psum.tile([P, 4, P], F32, name="tp_x%d_%d" % (n, kk), tag="ps")
                 for k2 in range(2):
                     for u in range(2):
                         k = 2 * kk + k2
                         nc.tensor.transpose(tp[:, 2 * k2 + u, :], words[:, 256 * k + u : 256 * (k + 1) : 2], ident[:])
-                if keep:
-                    dummy(idle, KEEP_N)
                 engines[kk](
                     out=gw[:, 2 * kk : 2 * kk + 2, :, :],
                     in_=tp[:].rearrange("p (k u) b -> p k b u", u=2),
@@ -234,15 +221,12 @@ def tile_butterflyblocksparselinear_kernel(tc, x, factorL, factorR, bias, out):
                     in_=o_sb[n][:].rearrange("p s l -> p (s l)"),
                 )
 
-        load_x(0, 2)
+        load_x(0, 4)
         for rt in range(4):
             load_w("fl%d" % rt, fl_rows[rt])
         load_x(1, 1)
 
-        first = psum.tile([P, 512], F32, name="first", tag="ps")
-        for w in range(WARM_UP):
-            dummy(first, 512)
-        turn_x(0, [act, dve, act, dve], True)
+        turn_x(0, [act, dve, act, dve])
         quant_x(0)
         for rt in range(4):
             grouped = prep_fl(rt)
@@ -251,20 +235,24 @@ def tile_butterflyblocksparselinear_kernel(tc, x, factorL, factorR, bias, out):
         load_x(2, 1)
         nc.sync.dma_start(out=bias_bc[:].rearrange("p s l -> p (s l)"), in_=bias.partition_broadcast(P))
         load_x(3, 1)
-        turn_x(1, [act, dve, act, dve], True)
+        turn_x(1, [act, dve, act, dve])
         quant_x(1)
         load_x(4, 1)
         load_x(5, 1)
-        for c in range(4):
+        for k in range(4):
+            stage1(0, k, act if k % 2 == 0 else dve)
+        grouped = prep_fr(0)
+        quant_fr(0, grouped)
+        for k in range(4, 8):
+            stage1(0, k, act if k % 2 == 0 else dve)
+        for c in range(1, 4):
             grouped = prep_fr(c)
             quant_fr(c, grouped)
-            stage1(0, 2 * c, act)
-            stage1(0, 2 * c + 1, dve)
 
         for i in range(NBT):
             turn_h(i)
             if i + 2 < NBT:
-                turn_x(i + 2, [act, dve, act, dve], False)
+                turn_x(i + 2, [act, act, act, act])
                 if i + 6 < NBT:
                     load_x(i + 6, 1)
             for j in range(8 + LEAD):

from contextlib import ExitStack

import concourse.mybir as mybir
from concourse.masks import make_identity

F32 = mybir.dt.float32
BF16 = mybir.dt.bfloat16
U32 = mybir.dt.uint32
U8 = mybir.dt.uint8
FP8X4 = mybir.dt.float8_e4m3fn_x4
ADD = mybir.AluOpType.add

H_BANK = F32

P = 128
NBT = 8
NK = 8
NL = 8
FLOPS = 2 * 2 * 1024 * 4096 * 512
LEAD = 2


def tile_butterflyblocksparselinear_kernel(tc, x, factorL, factorR, bias, out):
    nc = tc.nc
    xf = x.flatten_outer_dims()
    of = out.flatten_outer_dims()
    fl_rows = factorL.rearrange("k q p -> (k q) p").rearrange("(t r l) p -> t r l p", r=P, l=8)
    fr_rows = factorR.rearrange("l s r -> (l s) r").rearrange("(c g s) r -> c s g r", g=8, s=P)

    with ExitStack() as ctx:
        const = ctx.enter_context(tc.tile_pool(name="const", bufs=1))
        wraw_pool = ctx.enter_context(tc.tile_pool(name="wraw", bufs=4))
        wg_pool = ctx.enter_context(tc.tile_pool(name="wg", bufs=2))
        xraw_pool = ctx.enter_context(tc.tile_pool(name="xraw", bufs=4))
        two = ctx.enter_context(tc.tile_pool(name="two", bufs=2))
        three = ctx.enter_context(tc.tile_pool(name="three", bufs=3))
        o_pool = ctx.enter_context(tc.tile_pool(name="o", bufs=4))
        psum = ctx.enter_context(tc.psum_pool(name="psum", bufs=8))
        ctx.enter_context(tc.manual_schedule())

        act = nc.scalar.copy
        dve = nc.vector.tensor_copy

        warm_in = const.tile([P, 1], F32, name="warm_in", tag="warm_in")
        warm_out = const.tile([P, 1], F32, name="warm_out", tag="warm_out")
        nc.vector.memset(warm_in[:], 0.0)
        nc.scalar.copy(out=warm_out[:], in_=warm_in[:])
        ident = const.tile([P, P], F32, name="ident", tag="ident")
        make_identity(nc, ident[:])
        perm = const.tile([P, P], F32, name="perm", tag="perm")
        for k2 in range(2):
            nc.vector.tensor_copy(
                out=perm[:, 64 * k2 : 64 * k2 + 64].rearrange("p (u c e) -> p u c e", u=2, e=2),
                in_=ident[:, 64 * k2 : 64 * k2 + 64].rearrange("p (c u e) -> p u c e", u=2, e=2),
            )
        bias_bc = const.tile([P, 512, 8], BF16, name="bias_bc", tag="bias_bc")
        fl_q = const.tile([P, NK, 512], U32, name="fl_q", tag="fl_q", align_bytes=64)
        fl_s = const.tile([P, NK, 512], U8, name="fl_s", tag="fl_s", align_bytes=64)
        fr_q = const.tile([P, NL, 512], U32, name="fr_q", tag="fr_q", align_bytes=64)
        fr_s = const.tile([P, NL, 512], U8, name="fr_s", tag="fr_s", align_bytes=64)

        x_raw = {}
        x_g = {}
        x_q = {}
        x_s = {}
        w_raw = {}
        g_nat = {}
        g_g = {}
        g_q = {}
        g_s = {}
        o_sb = {}

        def load_x(n, pieces):
            x_raw[n] = xraw_pool.tile([P, 4096], BF16, name="x_raw%d" % n, tag="x_raw")
            w = 4096 // pieces
            for c in range(pieces):
                nc.sync.dma_start(
                    out=x_raw[n][:, c * w : (c + 1) * w],
                    in_=xf[P * n : P * (n + 1), c * w : (c + 1) * w],
                )

        def load_w(key, rows):
            w_raw[key] = wraw_pool.tile([P, 8, 512], BF16, name="w_raw_%s" % key, tag="w_raw")
            nc.sync.dma_start(out=w_raw[key][:], in_=rows)

        def quantize(src, codes, scales):
            nc.vector.quantize_mx(out=codes.bitcast(FP8X4), scales=scales, in_=src)

        def prep_fl(rt):
            words = w_raw["fl%d" % rt][:].bitcast(F32)
            grouped = wg_pool.tile([P, 2, 8, 64, 4], BF16, name="fl_g%d" % rt, tag="w_g", align_bytes=64)
            gw = grouped[:].bitcast(F32)
            for ll in range(4):
                tp = psum.tile([P, 4, P], F32, name="tp_fl%d_%d" % (rt, ll), tag="ps")
                for l2 in range(2):
                    for u in range(2):
                        nc.tensor.transpose(tp[:, 2 * l2 + u, :], words[:, 2 * ll + l2, u:256:2], perm[:])
                act(
                    out=gw[:, :, 2 * ll : 2 * ll + 2, :, :],
                    in_=tp[:].rearrange("p (l u) (k n) -> p k l n u", u=2, k=2),
                )
            return grouped

        def quant_fl(rt, grouped):
            for k2 in range(2):
                quantize(
                    grouped[:, k2].rearrange("p l n t -> p (l n t)"),
                    fl_q[:, 2 * rt + k2, :],
                    fl_s[:, 2 * rt + k2, :],
                )

        def prep_fr(c):
            words = w_raw["fr%d" % c][:].bitcast(F32)
            grouped = wg_pool.tile([P, 2, 512, 4], BF16, name="fr_g%d" % c, tag="w_g", align_bytes=64)
            gw = grouped[:].bitcast(F32)
            for l2 in range(2):
                for ah in range(2):
                    tp = psum.tile([P, 4, P], F32, name="tp_fr%d_%d_%d" % (c, l2, ah), tag="ps")
                    for a2 in range(2):
                        for u in range(2):
                            nc.tensor.transpose(
                                tp[:, 2 * a2 + u, :], words[:, 4 * l2 + 2 * ah + a2, u:256:2], ident[:]
                            )
                    act(
                        out=gw[:, l2, 256 * ah : 256 * ah + 256, :].rearrange("p (a s) u -> p a s u", a=2),
                        in_=tp[:].rearrange("p (a u) s -> p a s u", u=2),
                    )
            return grouped

        def quant_fr(c, grouped):
            for l2 in range(2):
                quantize(
                    grouped[:, l2].rearrange("p s t -> p (s t)"),
                    fr_q[:, 2 * c + l2, :],
                    fr_s[:, 2 * c + l2, :],
                )

        def turn_x(n, engines):
            words = x_raw[n][:].bitcast(F32)
            x_g[n] = two.tile([P, NK, P, 4], BF16, name="x_g%d" % n, tag="x_g", align_bytes=64)
            x_q[n] = three.tile([P, NK * P], U32, name="x_q%d" % n, tag="x_q", align_bytes=64)
            x_s[n] = three.tile([P, NK * P], U8, name="x_s%d" % n, tag="x_s", align_bytes=64)
            gw = x_g[n][:].bitcast(F32)
            for kk in range(4):
                tp = psum.tile([P, 4, P], F32, name="tp_x%d_%d" % (n, kk), tag="ps")
                for k2 in range(2):
                    for u in range(2):
                        k = 2 * kk + k2
                        nc.tensor.transpose(tp[:, 2 * k2 + u, :], words[:, 256 * k + u : 256 * (k + 1) : 2], ident[:])
                engines[kk](
                    out=gw[:, 2 * kk : 2 * kk + 2, :, :],
                    in_=tp[:].rearrange("p (k u) b -> p k b u", u=2),
                )

        def quant_x(n):
            quantize(x_g[n][:].rearrange("p k b t -> p (k b t)"), x_q[n][:], x_s[n][:])

        def stage1(n, k, eng):
            if k == 0:
                g_nat[n] = two.tile([P, 16, NK, 32], BF16, name="g_nat%d" % n, tag="g_nat")
            h_ps = psum.tile([P, 512], H_BANK, name="h_ps%d_%d" % (n, k), tag="ps")
            nc.tensor.matmul_mx(
                out=h_ps[:],
                lhsT=x_q[n][:, P * k : P * (k + 1)].bitcast(FP8X4),
                lhsT_scale=x_s[n][:, P * k : P * (k + 1)],
                rhs=fl_q[:, k, :].bitcast(FP8X4),
                rhs_scale=fl_s[:, k, :],
                start=True,
                stop=True,
            )
            eng(out=g_nat[n][:, :, k, :], in_=h_ps[:].rearrange("p (a c) -> p a c", c=32))

        def turn_h(n):
            words = g_nat[n][:].rearrange("p a k c -> p (a k c)").bitcast(F32)
            g_g[n] = two.tile([P, NL, P, 4], BF16, name="g_g%d" % n, tag="g_g", align_bytes=64)
            g_q[n] = two.tile([P, NL * P], U32, name="g_q%d" % n, tag="g_q", align_bytes=64)
            g_s[n] = two.tile([P, NL * P], U8, name="g_s%d" % n, tag="g_s", align_bytes=64)
            gw = g_g[n][:].bitcast(F32)
            for ll in range(4):
                tp = psum.tile([P, 4, P], F32, name="tp_h%d_%d" % (n, ll), tag="ps")
                for s in range(4):
                    nc.tensor.transpose(tp[:, s, :], words[:, P * (4 * ll + s) : P * (4 * ll + s + 1)], ident[:])
                act(
                    out=gw[:, 2 * ll : 2 * ll + 2, :, :],
                    in_=tp[:].rearrange("p (l u) b -> p l b u", u=2),
                )
                if ll % 2 == 1:
                    h = ll // 2
                    quantize(
                        g_g[n][:, 4 * h : 4 * h + 4, :, :].rearrange("p l b t -> p (l b t)"),
                        g_q[n][:, 512 * h : 512 * h + 512],
                        g_s[n][:, 512 * h : 512 * h + 512],
                    )

        def stage2(n, j):
            a = j // 2
            lh = j % 2
            if lh == 0:
                o_sb[n] = o_pool.tile([P, P, 8], F32, name="o_sb%d_%d" % (n, a), tag="o_sb")
            y_ps = psum.tile([P, 4, P], F32, name="y_ps%d_%d" % (n, j), tag="ps")
            for l4 in range(4):
                l = 4 * lh + l4
                nc.tensor.matmul_mx(
                    out=y_ps[:, l4, :],
                    lhsT=g_q[n][:, P * l : P * (l + 1)].bitcast(FP8X4),
                    lhsT_scale=g_s[n][:, P * l : P * (l + 1)],
                    rhs=fr_q[:, l, P * a : P * (a + 1)].bitcast(FP8X4),
                    rhs_scale=fr_s[:, l, P * a : P * (a + 1)],
                    start=True,
                    stop=True,
                )
            nc.vector.tensor_tensor(
                out=o_sb[n][:, :, 4 * lh : 4 * lh + 4],
                in0=y_ps[:].rearrange("p l s -> p s l"),
                in1=bias_bc[:, P * a : P * (a + 1), 4 * lh : 4 * lh + 4],
                op=ADD,
            )
            if lh == 1:
                nc.sync.dma_start(
                    out=of[P * n : P * (n + 1), 1024 * a : 1024 * (a + 1)],
                    in_=o_sb[n][:].rearrange("p s l -> p (s l)"),
                )

        load_x(0, 4)
        for rt in range(4):
            load_w("fl%d" % rt, fl_rows[rt])
        load_x(1, 1)

        turn_x(0, [act, dve, act, dve])
        quant_x(0)
        for rt in range(4):
            grouped = prep_fl(rt)
            load_w("fr%d" % rt, fr_rows[rt])
            quant_fl(rt, grouped)
        load_x(2, 1)
        nc.sync.dma_start(out=bias_bc[:].rearrange("p s l -> p (s l)"), in_=bias.partition_broadcast(P))
        load_x(3, 1)
        turn_x(1, [act, dve, act, dve])
        quant_x(1)
        load_x(4, 1)
        load_x(5, 1)
        for k in range(4):
            stage1(0, k, act if k % 2 == 0 else dve)
        grouped = prep_fr(0)
        quant_fr(0, grouped)
        for k in range(4, 8):
            stage1(0, k, act if k % 2 == 0 else dve)
        for c in range(1, 4):
            grouped = prep_fr(c)
            quant_fr(c, grouped)

        for i in range(NBT):
            turn_h(i)
            if i + 2 < NBT:
                turn_x(i + 2, [act, act, act, act])
                if i + 6 < NBT:
                    load_x(i + 6, 1)
            for j in range(8 + LEAD):
                if j < 8 and i + 1 < NBT:
                    stage1(i + 1, j, act)
                if j >= LEAD:
                    stage2(i, j - LEAD)
                    if i + 2 < NBT and j - LEAD == 2:
                        quant_x(i + 2)
